import numpy as np
import ml_dtypes


def mxq(x, axis, fmt="e4m3"):
    dtype, down = {"e4m3": (ml_dtypes.float8_e4m3fn, 7), "e5m2": (ml_dtypes.float8_e5m2, 14)}[fmt]
    v = np.moveaxis(np.asarray(x, np.float32).astype(ml_dtypes.bfloat16).astype(np.float64), axis, -1)
    blocks = v.reshape(v.shape[:-1] + (-1, 32))
    amax = np.abs(blocks).max(-1, keepdims=True)
    byte = np.maximum(np.where(amax > 0, np.frexp(amax)[1] - 1 + 127, 0) - down, 1)
    scale = np.exp2(byte - 127.0)
    codes = (blocks / scale).astype(np.float32).astype(dtype).astype(np.float64)
    return np.moveaxis((codes * scale).reshape(v.shape), -1, axis)


WIDE = False


def mx_kscale(k):
    if not WIDE:
        return np.ones(k)
    levels = np.array([10, -10, 5, -5, 0])
    a = np.random.permutation(np.resize(levels, k // 512 * 4)).reshape(k // 512, 4)
    idx = np.arange(k)
    return np.exp2(a[idx // 512, idx % 128 // 32])


BF16 = ml_dtypes.bfloat16


def bf(x):
    return np.asarray(x, np.float32).astype(BF16)


def f64(x):
    return np.asarray(x).astype(np.float64)


B, S, H, E, V, G, P = 1, 128, 1024, 512, 768, 1, 1
C = G + P
KNOTS = np.linspace(-1.0 - 2.0 / G * P, 1.0 + 2.0 / G * P, G + 2 * P + 1)


def silu(v):
    e = np.exp(-np.abs(v))
    return v * np.where(v >= 0.0, 1.0, e) / (1.0 + e)


def b_splines(x):
    xe = x[..., None]
    bases = np.where((xe >= KNOTS[:-1]) & (xe < KNOTS[1:]), 1.0, 0.0)
    for p in range(1, P + 1):
        left = (xe - KNOTS[: -(p + 1)]) / (KNOTS[p:-1] - KNOTS[: -(p + 1)])
        right = (KNOTS[p + 1:] - xe) / (KNOTS[p + 1:] - KNOTS[1:-p])
        bases = left * bases[..., :-1] + right * bases[..., 1:]
    return bases


def setup_inputs():
    s = mx_kscale(E)
    u = s / s.min()
    return {"h_norm": bf(np.random.standard_normal((B, S, E)) * u),
            "base_w2": bf(np.random.standard_normal((V, E)) / np.sqrt(E) / u),
            "spline_w2": bf(np.random.standard_normal((V, E, C)) / np.sqrt(E))}


def reference(h_norm, base_w2, spline_w2):
    x = f64(h_norm).reshape(B * S, E)
    base = mxq(silu(x), 1, "e4m3") @ mxq(f64(base_w2), 1, "e4m3").T
    spl = mxq(b_splines(x).reshape(B * S, E * C), 1, "e4m3") @ mxq(f64(spline_w2).reshape(V, E * C), 1, "e4m3").T
    return (base + spl).reshape(B, S, V)

@@ -1,0 +1,153 @@
+from contextlib import ExitStack
+
+import concourse.mybir as mybir
+from concourse.masks import make_identity
+
+BF16 = mybir.dt.bfloat16
+F32 = mybir.dt.float32
+U32 = mybir.dt.uint32
+U8 = mybir.dt.uint8
+FP8X4 = mybir.dt.float8_e4m3fn_x4
+ACT = mybir.ActivationFunctionType
+
+P = 128
+FEATURES = 512
+OUTPUTS = 768
+BASES = 2
+PACK = 4
+HALVES = 2
+PASS_WORDS = HALVES * P
+PASSES = 3
+BASE_PASS = 2
+GROUP = 256
+GROUPS = OUTPUTS // GROUP
+ROWS = GROUP // P
+CENTRES = (-1.0, 1.0)
+HAT_SLOPE = 0.5
+
+FLOPS = 2 * P * OUTPUTS * FEATURES * (1 + BASES)
+
+
+def tile_generatorhead_pb_s_kernel(tc, h_norm, base_w2, spline_w2, out):
+    nc = tc.nc
+    x_dram = h_norm.flatten_outer_dims()
+    out_dram = out.flatten_outer_dims()
+
+    with ExitStack() as ctx:
+        consts = ctx.enter_context(tc.tile_pool(name="consts", bufs=1))
+        loaded = ctx.enter_context(tc.tile_pool(name="loaded", bufs=1))
+        keep = ctx.enter_context(tc.tile_pool(name="keep", bufs=1))
+        stage = ctx.enter_context(tc.tile_pool(name="stage", bufs=4))
+        banks = ctx.enter_context(tc.psum_pool(name="banks", bufs=5))
+        sums = ctx.enter_context(tc.psum_pool(name="sums", bufs=GROUPS))
+        ctx.enter_context(tc.manual_schedule())
+
+        x_rows = loaded.tile([P, FEATURES], BF16, name="x_rows")
+        nc.sync.dma_start(out=x_rows[:], in_=x_dram)
+        spline_rows = []
+        base_rows = []
+        for g in range(GROUPS):
+            outputs = slice(g * GROUP, (g + 1) * GROUP)
+            spline_g = loaded.tile([P, ROWS * FEATURES * BASES], BF16, name="spline_rows%d" % g)
+            nc.sync.dma_start(out=spline_g[:], in_=spline_w2[outputs, :, :].rearrange("(p r) i c -> p (r i c)", r=ROWS))
+            spline_rows.append(spline_g)
+            base_g = loaded.tile([P, ROWS * FEATURES], BF16, name="base_rows%d" % g)
+            nc.sync.dma_start(out=base_g[:], in_=base_w2[outputs, :].rearrange("(p r) i -> p (r i)", r=ROWS))
+            base_rows.append(base_g)
+
+        ident_f32 = consts.tile([P, P], F32, name="ident_f32")
+        make_identity(nc, ident_f32[:])
+        ident_bf16 = consts.tile([P, P], BF16, name="ident_bf16")
+        make_identity(nc, ident_bf16[:])
+        minus_centre = consts.tile([P, BASES], F32, name="minus_centre")
+        for c in range(BASES):
+            nc.vector.memset(minus_centre[:, c : c + 1], -CENTRES[c])
+        one = consts.tile([P, 1], F32, name="one")
+        nc.vector.memset(one[:], 1.0)
+
+        x_words = banks.tile([P, HALVES * P], F32, tag="bank", name="x_words")
+        for u in range(HALVES):
+            nc.tensor.transpose(x_words[:, u * P : (u + 1) * P], x_rows[:].bitcast(F32)[:, u * P : (u + 1) * P], ident_f32[:])
+        x_cols = banks.tile([P, FEATURES], BF16, tag="bank", name="x_cols")
+        for j in range(FEATURES // P):
+            nc.tensor.transpose(x_cols[:, j * P : (j + 1) * P], x_rows[:, j * P : (j + 1) * P], ident_bf16[:])
+
+        silu_grouped = keep.tile([P, P * PACK], BF16, name="silu_grouped", align_bytes=64)
+        nc.scalar.activation(
+            out=silu_grouped[:].rearrange("p (t u e) -> p t u e", u=HALVES, e=2),
+            in_=x_words[:].bitcast(BF16).rearrange("p (u t e) -> p t u e", u=HALVES, e=2),
+            func=ACT.Silu,
+        )
+        distance = keep.tile([P, BASES, FEATURES], F32, name="distance")
+        for c in range(BASES):
+            nc.scalar.activation(
+                out=distance[:, c, :].rearrange("p (s t u) -> p s t u", t=P, u=HALVES),
+                in_=x_cols[:].rearrange("p (s u t) -> p s t u", t=P, u=HALVES),
+                func=ACT.Abs,
+                bias=minus_centre[:, c : c + 1],
+            )
+        hats_grouped = keep.tile([P, FEATURES * BASES], BF16, name="hats_grouped", align_bytes=64)
+        nc.scalar.activation(
+            out=hats_grouped[:].rearrange("p (n c) -> p n c", c=BASES),
+            in_=distance[:].rearrange("p c n -> p n c"),
+            func=ACT.Relu,
+            scale=-HAT_SLOPE,
+            bias=one[:],
+        )
+
+        x_codes = keep.tile([P, PASSES * P], U32, name="x_codes", align_bytes=64)
+        x_scales = keep.tile([P, PASSES * P], U8, name="x_scales", align_bytes=64)
+
+        def quantise_x():
+            spline_cols = slice(0, BASE_PASS * P)
+            base_cols = slice(BASE_PASS * P, PASSES * P)
+            nc.vector.quantize_mx(out=x_codes[:, spline_cols].bitcast(FP8X4), scales=x_scales[:, spline_cols], in_=hats_grouped[:])
+            nc.vector.quantize_mx(out=x_codes[:, base_cols].bitcast(FP8X4), scales=x_scales[:, base_cols], in_=silu_grouped[:])
+
+        w_codes = keep.tile([P, GROUPS, PASSES, GROUP], U32, name="w_codes", align_bytes=64)
+        w_scales = keep.tile([P, GROUPS, PASSES, GROUP], U8, name="w_scales", align_bytes=64)
+
+        def pass_words(g, c):
+            if c == BASE_PASS:
+                return base_rows[g][:].bitcast(F32).rearrange("p (r w) -> p r w", r=ROWS)
+            words = spline_rows[g][:].bitcast(F32).rearrange("p (r w) -> p r w", r=ROWS)
+            return words[:, :, c * PASS_WORDS : (c + 1) * PASS_WORDS]
+
+        def prepare_group(g, copy_out):
+            grouped = []
+            for c in range(PASSES):
+                words = pass_words(g, c)
+                bank = banks.tile([P, ROWS * HALVES, P], F32, tag="bank", name="bank")
+                for r in range(ROWS):
+                    for u in range(HALVES):
+                        nc.tensor.transpose(bank[:, r * HALVES + u, :], words[:, r, u * P : (u + 1) * P], ident_f32[:])
+                grouped_c = stage.tile([P, GROUP * PACK], BF16, tag="grouped", name="grouped", align_bytes=64)
+                copy_out(
+                    out=grouped_c[:].bitcast(F32).rearrange("k (p h) -> k p h", h=ROWS * HALVES),
+                    in_=bank[:].rearrange("k h p -> k p h"),
+                )
+                grouped.append(grouped_c)
+                if c > 0:
+                    nc.vector.quantize_mx(out=w_codes[:, g, c - 1, :].bitcast(FP8X4), scales=w_scales[:, g, c - 1, :], in_=grouped[c - 1][:])
+            nc.vector.quantize_mx(out=w_codes[:, g, PASSES - 1, :].bitcast(FP8X4), scales=w_scales[:, g, PASSES - 1, :], in_=grouped[PASSES - 1][:])
+
+        prepare_group(0, nc.vector.tensor_copy)
+        quantise_x()
+        for g in range(1, GROUPS):
+            prepare_group(g, nc.scalar.copy)
+
+        for g in range(GROUPS):
+            acc = sums.tile([P, GROUP], F32, tag="acc", name="acc")
+            for c in range(PASSES):
+                nc.tensor.matmul_mx(
+                    out=acc[:],
+                    lhsT=x_codes[:, c * P : (c + 1) * P].bitcast(FP8X4),
+                    lhsT_scale=x_scales[:, c * P : (c + 1) * P],
+                    rhs=w_codes[:, g, c, :].bitcast(FP8X4),
+                    rhs_scale=w_scales[:, g, c, :],
+                    start=(c == 0),
+                    stop=(c == PASSES - 1),
+                )
+            result = stage.tile([P, GROUP], F32, tag="result", name="result")
+            nc.scalar.copy(out=result[:], in_=acc[:])
+            nc.sync.dma_start(out=out_dram[:, g * GROUP : (g + 1) * GROUP], in_=result[:])

@@ -24,6 +24,9 @@ GROUPS = OUTPUTS // GROUP
 ROWS = GROUP // P
 CENTRES = (-1.0, 1.0)
 HAT_SLOPE = 0.5
+WARM_PASSES = 6
+HOLD_PASSES = 4
+I32 = mybir.dt.int32
 
 FLOPS = 2 * P * OUTPUTS * FEATURES * (1 + BASES)
 
@@ -38,7 +41,8 @@ def tile_generatorhead_pb_s_kernel(tc, h_norm, base_w2, spline_w2, out):
         loaded = ctx.enter_context(tc.tile_pool(name="loaded", bufs=1))
         keep = ctx.enter_context(tc.tile_pool(name="keep", bufs=1))
         stage = ctx.enter_context(tc.tile_pool(name="stage", bufs=4))
-        banks = ctx.enter_context(tc.psum_pool(name="banks", bufs=5))
+        banks = ctx.enter_context(tc.psum_pool(name="banks", bufs=4))
+        idle = ctx.enter_context(tc.psum_pool(name="idle", bufs=1))
         sums = ctx.enter_context(tc.psum_pool(name="sums", bufs=GROUPS))
         ctx.enter_context(tc.manual_schedule())
 
@@ -54,6 +58,27 @@ def tile_generatorhead_pb_s_kernel(tc, h_norm, base_w2, spline_w2, out):
             base_g = loaded.tile([P, ROWS * FEATURES], BF16, name="base_rows%d" % g)
             nc.sync.dma_start(out=base_g[:], in_=base_w2[outputs, :].rearrange("(p r) i -> p (r i)", r=ROWS))
             base_rows.append(base_g)
+
+        zeros = consts.tile([P, GROUP * PACK], BF16, name="zeros", align_bytes=64)
+        nc.vector.memset(zeros[:].bitcast(I32), 0)
+        zero_codes = consts.tile([P, GROUP], U32, name="zero_codes", align_bytes=64)
+        zero_scales = consts.tile([P, GROUP], U8, name="zero_scales", align_bytes=64)
+        nc.vector.quantize_mx(out=zero_codes[:].bitcast(FP8X4), scales=zero_scales[:], in_=zeros[:])
+        idle_sum = idle.tile([P, GROUP], F32, name="idle_sum")
+
+        def multiply_zeros(passes):
+            for i in range(passes):
+                nc.tensor.matmul_mx(
+                    out=idle_sum[:],
+                    lhsT=zero_codes[:, 0:P].bitcast(FP8X4),
+                    lhsT_scale=zero_scales[:, 0:P],
+                    rhs=zero_codes[:].bitcast(FP8X4),
+                    rhs_scale=zero_scales[:],
+                    start=True,
+                    stop=True,
+                )
+
+        multiply_zeros(WARM_PASSES)
 
         ident_f32 = consts.tile([P, P], F32, name="ident_f32")
         make_identity(nc, ident_f32[:])
@@ -71,6 +96,8 @@ def tile_generatorhead_pb_s_kernel(tc, h_norm, base_w2, spline_w2, out):
         x_cols = banks.tile([P, FEATURES], BF16, tag="bank", name="x_cols")
         for j in range(FEATURES // P):
             nc.tensor.transpose(x_cols[:, j * P : (j + 1) * P], x_rows[:, j * P : (j + 1) * P], ident_bf16[:])
+
+        multiply_zeros(HOLD_PASSES)
 
         silu_grouped = keep.tile([P, P * PACK], BF16, name="silu_grouped", align_bytes=64)
         nc.scalar.activation(
@@ -132,9 +159,11 @@ def tile_generatorhead_pb_s_kernel(tc, h_norm, base_w2, spline_w2, out):
             nc.vector.quantize_mx(out=w_codes[:, g, PASSES - 1, :].bitcast(FP8X4), scales=w_scales[:, g, PASSES - 1, :], in_=grouped[PASSES - 1][:])
 
         prepare_group(0, nc.vector.tensor_copy)
+        multiply_zeros(HOLD_PASSES)
         quantise_x()
-        for g in range(1, GROUPS):
-            prepare_group(g, nc.scalar.copy)
+        prepare_group(1, nc.scalar.copy)
+        multiply_zeros(HOLD_PASSES)
+        prepare_group(2, nc.scalar.copy)
 
         for g in range(GROUPS):
             acc = sums.tile([P, GROUP], F32, tag="acc", name="acc")

@@ -16,7 +16,6 @@ OUTPUTS = 768
 BASES = 2
 PACK = 4
 HALVES = 2
-PASS_WORDS = HALVES * P
 PASSES = 3
 BASE_PASS = 2
 GROUP = 256
@@ -24,9 +23,6 @@ GROUPS = OUTPUTS // GROUP
 ROWS = GROUP // P
 CENTRES = (-1.0, 1.0)
 HAT_SLOPE = 0.5
-WARM_PASSES = 6
-HOLD_PASSES = 4
-I32 = mybir.dt.int32
 
 FLOPS = 2 * P * OUTPUTS * FEATURES * (1 + BASES)
 
@@ -41,8 +37,7 @@ def tile_generatorhead_pb_s_kernel(tc, h_norm, base_w2, spline_w2, out):
         loaded = ctx.enter_context(tc.tile_pool(name="loaded", bufs=1))
         keep = ctx.enter_context(tc.tile_pool(name="keep", bufs=1))
         stage = ctx.enter_context(tc.tile_pool(name="stage", bufs=4))
-        banks = ctx.enter_context(tc.psum_pool(name="banks", bufs=4))
-        idle = ctx.enter_context(tc.psum_pool(name="idle", bufs=1))
+        banks = ctx.enter_context(tc.psum_pool(name="banks", bufs=5))
         sums = ctx.enter_context(tc.psum_pool(name="sums", bufs=GROUPS))
         ctx.enter_context(tc.manual_schedule())
 
@@ -59,31 +54,8 @@ def tile_generatorhead_pb_s_kernel(tc, h_norm, base_w2, spline_w2, out):
             nc.sync.dma_start(out=base_g[:], in_=base_w2[outputs, :].rearrange("(p r) i -> p (r i)", r=ROWS))
             base_rows.append(base_g)
 
-        zeros = consts.tile([P, GROUP * PACK], BF16, name="zeros", align_bytes=64)
-        nc.vector.memset(zeros[:].bitcast(I32), 0)
-        zero_codes = consts.tile([P, GROUP], U32, name="zero_codes", align_bytes=64)
-        zero_scales = consts.tile([P, GROUP], U8, name="zero_scales", align_bytes=64)
-        nc.vector.quantize_mx(out=zero_codes[:].bitcast(FP8X4), scales=zero_scales[:], in_=zeros[:])
-        idle_sum = idle.tile([P, GROUP], F32, name="idle_sum")
-
-        def multiply_zeros(passes):
-            for i in range(passes):
-                nc.tensor.matmul_mx(
-                    out=idle_sum[:],
-                    lhsT=zero_codes[:, 0:P].bitcast(FP8X4),
-                    lhsT_scale=zero_scales[:, 0:P],
-                    rhs=zero_codes[:].bitcast(FP8X4),
-                    rhs_scale=zero_scales[:],
-                    start=True,
-                    stop=True,
-                )
-
-        multiply_zeros(WARM_PASSES)
-
         ident_f32 = consts.tile([P, P], F32, name="ident_f32")
         make_identity(nc, ident_f32[:])
-        ident_bf16 = consts.tile([P, P], BF16, name="ident_bf16")
-        make_identity(nc, ident_bf16[:])
         minus_centre = consts.tile([P, BASES], F32, name="minus_centre")
         for c in range(BASES):
             nc.vector.memset(minus_centre[:, c : c + 1], -CENTRES[c])
@@ -93,11 +65,6 @@ def tile_generatorhead_pb_s_kernel(tc, h_norm, base_w2, spline_w2, out):
         x_words = banks.tile([P, HALVES * P], F32, tag="bank", name="x_words")
         for u in range(HALVES):
             nc.tensor.transpose(x_words[:, u * P : (u + 1) * P], x_rows[:].bitcast(F32)[:, u * P : (u + 1) * P], ident_f32[:])
-        x_cols = banks.tile([P, FEATURES], BF16, tag="bank", name="x_cols")
-        for j in range(FEATURES // P):
-            nc.tensor.transpose(x_cols[:, j * P : (j + 1) * P], x_rows[:, j * P : (j + 1) * P], ident_bf16[:])
-
-        multiply_zeros(HOLD_PASSES)
 
         silu_grouped = keep.tile([P, P * PACK], BF16, name="silu_grouped", align_bytes=64)
         nc.scalar.activation(
@@ -107,12 +74,7 @@ def tile_generatorhead_pb_s_kernel(tc, h_norm, base_w2, spline_w2, out):
         )
         distance = keep.tile([P, BASES, FEATURES], F32, name="distance")
         for c in range(BASES):
-            nc.scalar.activation(
-                out=distance[:, c, :].rearrange("p (s t u) -> p s t u", t=P, u=HALVES),
-                in_=x_cols[:].rearrange("p (s u t) -> p s t u", t=P, u=HALVES),
-                func=ACT.Abs,
-                bias=minus_centre[:, c : c + 1],
-            )
+            nc.scalar.activation(out=distance[:, c, :], in_=x_words[:].bitcast(BF16), func=ACT.Abs, bias=minus_centre[:, c : c + 1])
         hats_grouped = keep.tile([P, FEATURES * BASES], BF16, name="hats_grouped", align_bytes=64)
         nc.scalar.activation(
             out=hats_grouped[:].rearrange("p (n c) -> p n c", c=BASES),
@@ -136,9 +98,9 @@ def tile_generatorhead_pb_s_kernel(tc, h_norm, base_w2, spline_w2, out):
 
         def pass_words(g, c):
             if c == BASE_PASS:
-                return base_rows[g][:].bitcast(F32).rearrange("p (r w) -> p r w", r=ROWS)
-            words = spline_rows[g][:].bitcast(F32).rearrange("p (r w) -> p r w", r=ROWS)
-            return words[:, :, c * PASS_WORDS : (c + 1) * PASS_WORDS]
+                return base_rows[g][:].bitcast(F32).rearrange("p (r h k) -> p r h k", r=ROWS, h=HALVES)
+            words = spline_rows[g][:].bitcast(F32).rearrange("p (r s k h) -> p r s h k", r=ROWS, k=P, h=HALVES)
+            return words[:, :, c, :, :]
 
         def prepare_group(g, copy_out):
             grouped = []
@@ -146,8 +108,8 @@ def tile_generatorhead_pb_s_kernel(tc, h_norm, base_w2, spline_w2, out):
                 words = pass_words(g, c)
                 bank = banks.tile([P, ROWS * HALVES, P], F32, tag="bank", name="bank")
                 for r in range(ROWS):
-                    for u in range(HALVES):
-                        nc.tensor.transpose(bank[:, r * HALVES + u, :], words[:, r, u * P : (u + 1) * P], ident_f32[:])
+                    for h in range(HALVES):
+                        nc.tensor.transpose(bank[:, r * HALVES + h, :], words[:, r, h, :], ident_f32[:])
                 grouped_c = stage.tile([P, GROUP * PACK], BF16, tag="grouped", name="grouped", align_bytes=64)
                 copy_out(
                     out=grouped_c[:].bitcast(F32).rearrange("k (p h) -> k p h", h=ROWS * HALVES),
@@ -159,11 +121,9 @@ def tile_generatorhead_pb_s_kernel(tc, h_norm, base_w2, spline_w2, out):
             nc.vector.quantize_mx(out=w_codes[:, g, PASSES - 1, :].bitcast(FP8X4), scales=w_scales[:, g, PASSES - 1, :], in_=grouped[PASSES - 1][:])
 
         prepare_group(0, nc.vector.tensor_copy)
-        multiply_zeros(HOLD_PASSES)
         quantise_x()
-        prepare_group(1, nc.scalar.copy)
-        multiply_zeros(HOLD_PASSES)
-        prepare_group(2, nc.scalar.copy)
+        for g in range(1, GROUPS):
+            prepare_group(g, nc.scalar.copy)
 
         for g in range(GROUPS):
             acc = sums.tile([P, GROUP], F32, tag="acc", name="acc")

@@ -16,11 +16,10 @@ OUTPUTS = 768
 BASES = 2
 PACK = 4
 HALVES = 2
+SPLINE_PASSES = 2
 PASSES = 3
-BASE_PASS = 2
-GROUP = 256
-GROUPS = OUTPUTS // GROUP
-ROWS = GROUP // P
+TILES = OUTPUTS // P
+PAIRS = TILES // 2
 CENTRES = (-1.0, 1.0)
 HAT_SLOPE = 0.5
 
@@ -36,23 +35,29 @@ def tile_generatorhead_pb_s_kernel(tc, h_norm, base_w2, spline_w2, out):
         consts = ctx.enter_context(tc.tile_pool(name="consts", bufs=1))
         loaded = ctx.enter_context(tc.tile_pool(name="loaded", bufs=1))
         keep = ctx.enter_context(tc.tile_pool(name="keep", bufs=1))
-        stage = ctx.enter_context(tc.tile_pool(name="stage", bufs=4))
-        banks = ctx.enter_context(tc.psum_pool(name="banks", bufs=5))
-        sums = ctx.enter_context(tc.psum_pool(name="sums", bufs=GROUPS))
+        banks = ctx.enter_context(tc.psum_pool(name="banks", bufs=4))
+        sums = ctx.enter_context(tc.psum_pool(name="sums", bufs=4))
         ctx.enter_context(tc.manual_schedule())
 
         x_rows = loaded.tile([P, FEATURES], BF16, name="x_rows")
         nc.sync.dma_start(out=x_rows[:], in_=x_dram)
-        spline_rows = []
-        base_rows = []
-        for g in range(GROUPS):
-            outputs = slice(g * GROUP, (g + 1) * GROUP)
-            spline_g = loaded.tile([P, ROWS * FEATURES * BASES], BF16, name="spline_rows%d" % g)
-            nc.sync.dma_start(out=spline_g[:], in_=spline_w2[outputs, :, :].rearrange("(p r) i c -> p (r i c)", r=ROWS))
-            spline_rows.append(spline_g)
-            base_g = loaded.tile([P, ROWS * FEATURES], BF16, name="base_rows%d" % g)
-            nc.sync.dma_start(out=base_g[:], in_=base_w2[outputs, :].rearrange("(p r) i -> p (r i)", r=ROWS))
-            base_rows.append(base_g)
+        spline_rows = {}
+        base_rows = {}
+        for q in range(PAIRS):
+            for j in (2 * q, 2 * q + 1):
+                rows = loaded.tile([P, FEATURES * BASES], BF16, name="spline_rows%d" % j)
+                nc.sync.dma_start(out=rows[:], in_=spline_w2[j * P : (j + 1) * P, :, :].rearrange("p i c -> p (i c)"))
+                spline_rows[j] = rows
+            if q < PAIRS - 1:
+                rows = loaded.tile([P, 2, FEATURES], BF16, name="base_rows%d" % q)
+                nc.sync.dma_start(out=rows[:], in_=base_w2[2 * q * P : (2 * q + 2) * P, :].rearrange("(r p) i -> p r i", p=P))
+                base_rows[2 * q] = rows[:, 0, :]
+                base_rows[2 * q + 1] = rows[:, 1, :]
+            else:
+                for j in (2 * q, 2 * q + 1):
+                    rows = loaded.tile([P, FEATURES], BF16, name="base_rows_tile%d" % j)
+                    nc.sync.dma_start(out=rows[:], in_=base_w2[j * P : (j + 1) * P, :])
+                    base_rows[j] = rows[:]
 
         ident_f32 = consts.tile([P, P], F32, name="ident_f32")
         make_identity(nc, ident_f32[:])
@@ -88,55 +93,113 @@ def tile_generatorhead_pb_s_kernel(tc, h_norm, base_w2, spline_w2, out):
         x_scales = keep.tile([P, PASSES * P], U8, name="x_scales", align_bytes=64)
 
         def quantise_x():
-            spline_cols = slice(0, BASE_PASS * P)
-            base_cols = slice(BASE_PASS * P, PASSES * P)
+            spline_cols = slice(0, SPLINE_PASSES * P)
+            base_cols = slice(SPLINE_PASSES * P, PASSES * P)
             nc.vector.quantize_mx(out=x_codes[:, spline_cols].bitcast(FP8X4), scales=x_scales[:, spline_cols], in_=hats_grouped[:])
             nc.vector.quantize_mx(out=x_codes[:, base_cols].bitcast(FP8X4), scales=x_scales[:, base_cols], in_=silu_grouped[:])
 
-        w_codes = keep.tile([P, GROUPS, PASSES, GROUP], U32, name="w_codes", align_bytes=64)
-        w_scales = keep.tile([P, GROUPS, PASSES, GROUP], U8, name="w_scales", align_bytes=64)
+        def spline_unit(j):
+            words = spline_rows[j][:].bitcast(F32).rearrange("p (s k h) -> p s h k", k=P, h=HALVES)
+            return [words[:, s, :, :] for s in range(SPLINE_PASSES)]
 
-        def pass_words(g, c):
-            if c == BASE_PASS:
-                return base_rows[g][:].bitcast(F32).rearrange("p (r h k) -> p r h k", r=ROWS, h=HALVES)
-            words = spline_rows[g][:].bitcast(F32).rearrange("p (r s k h) -> p r s h k", r=ROWS, k=P, h=HALVES)
-            return words[:, :, c, :, :]
+        def base_unit(tiles):
+            return [base_rows[j].bitcast(F32).rearrange("p (h k) -> p h k", h=HALVES) for j in tiles]
 
-        def prepare_group(g, copy_out):
-            grouped = []
-            for c in range(PASSES):
-                words = pass_words(g, c)
-                bank = banks.tile([P, ROWS * HALVES, P], F32, tag="bank", name="bank")
-                for r in range(ROWS):
-                    for h in range(HALVES):
-                        nc.tensor.transpose(bank[:, r * HALVES + h, :], words[:, r, h, :], ident_f32[:])
-                grouped_c = stage.tile([P, GROUP * PACK], BF16, tag="grouped", name="grouped", align_bytes=64)
-                copy_out(
-                    out=grouped_c[:].bitcast(F32).rearrange("k (p h) -> k p h", h=ROWS * HALVES),
-                    in_=bank[:].rearrange("k h p -> k p h"),
-                )
-                grouped.append(grouped_c)
-                if c > 0:
-                    nc.vector.quantize_mx(out=w_codes[:, g, c - 1, :].bitcast(FP8X4), scales=w_scales[:, g, c - 1, :], in_=grouped[c - 1][:])
-            nc.vector.quantize_mx(out=w_codes[:, g, PASSES - 1, :].bitcast(FP8X4), scales=w_scales[:, g, PASSES - 1, :], in_=grouped[PASSES - 1][:])
+        def transpose_unit(blocks):
+            bank = banks.tile([P, len(blocks) * HALVES, P], F32, tag="bank", name="bank")
+            for b in range(len(blocks)):
+                for h in range(HALVES):
+                    nc.tensor.transpose(bank[:, b * HALVES + h, :], blocks[b][:, h, :], ident_f32[:])
+            return bank
 
-        prepare_group(0, nc.vector.tensor_copy)
+        def regroup_unit(copy_out, bank, name):
+            n = bank.shape[1] // HALVES
+            grouped = keep.tile([P, n * P * PACK], BF16, name="grouped_" + name, align_bytes=64)
+            copy_out(
+                out=grouped[:].bitcast(F32).rearrange("k (b p h) -> k b p h", b=n, h=HALVES),
+                in_=bank[:].rearrange("k (b h) p -> k b p h", h=HALVES),
+            )
+            return grouped
+
+        def quantise_unit(grouped, name):
+            n = grouped.shape[1] // PACK
+            codes = keep.tile([P, n], U32, name="codes_" + name, align_bytes=64)
+            scales = keep.tile([P, n], U8, name="scales_" + name, align_bytes=64)
+            nc.vector.quantize_mx(out=codes[:].bitcast(FP8X4), scales=scales[:], in_=grouped[:])
+            return codes, scales
+
+        def multiply(acc_cols, c, operand, b):
+            codes, scales = operand
+            nc.tensor.matmul_mx(
+                out=acc_cols,
+                lhsT=x_codes[:, c * P : (c + 1) * P].bitcast(FP8X4),
+                lhsT_scale=x_scales[:, c * P : (c + 1) * P],
+                rhs=codes[:, b * P : (b + 1) * P].bitcast(FP8X4),
+                rhs_scale=scales[:, b * P : (b + 1) * P],
+                start=(c == 0),
+                stop=(c == PASSES - 1),
+            )
+
+        vec = nc.vector.tensor_copy
+        sca = nc.scalar.copy
+
+        def multiply_pair(s_even, s_odd, b_both):
+            acc = sums.tile([P, 2 * P], F32, tag="acc", name="acc")
+            for r in range(2):
+                cols = acc[:, r * P : (r + 1) * P]
+                multiply(cols, 0, (s_even, s_odd)[r], 0)
+                multiply(cols, 1, (s_even, s_odd)[r], 1)
+                multiply(cols, 2, b_both, r)
+            return acc
+
+        def store(copy_out, acc, first):
+            width = acc.shape[1]
+            result = keep.tile([P, width], F32, name="result%d" % first)
+            copy_out(out=result[:], in_=acc[:])
+            nc.sync.dma_start(out=out_dram[:, first : first + width], in_=result[:])
+
+        bank = transpose_unit(spline_unit(0))
+        g_s0 = regroup_unit(vec, bank, "s0")
+        bank = transpose_unit(spline_unit(1))
+        g_s1 = regroup_unit(vec, bank, "s1")
+        s0 = quantise_unit(g_s0, "s0")
+        bank = transpose_unit(base_unit((0, 1)))
+        g_b0 = regroup_unit(vec, bank, "b0")
+        s1 = quantise_unit(g_s1, "s1")
+        b0 = quantise_unit(g_b0, "b0")
         quantise_x()
-        for g in range(1, GROUPS):
-            prepare_group(g, nc.scalar.copy)
-
-        for g in range(GROUPS):
-            acc = sums.tile([P, GROUP], F32, tag="acc", name="acc")
-            for c in range(PASSES):
-                nc.tensor.matmul_mx(
-                    out=acc[:],
-                    lhsT=x_codes[:, c * P : (c + 1) * P].bitcast(FP8X4),
-                    lhsT_scale=x_scales[:, c * P : (c + 1) * P],
-                    rhs=w_codes[:, g, c, :].bitcast(FP8X4),
-                    rhs_scale=w_scales[:, g, c, :],
-                    start=(c == 0),
-                    stop=(c == PASSES - 1),
-                )
-            result = stage.tile([P, GROUP], F32, tag="result", name="result")
-            nc.scalar.copy(out=result[:], in_=acc[:])
-            nc.sync.dma_start(out=out_dram[:, g * GROUP : (g + 1) * GROUP], in_=result[:])
+        bank = transpose_unit(spline_unit(2))
+        g_s2 = regroup_unit(sca, bank, "s2")
+        s2 = quantise_unit(g_s2, "s2")
+        bank = transpose_unit(spline_unit(3))
+        g_s3 = regroup_unit(sca, bank, "s3")
+        s3 = quantise_unit(g_s3, "s3")
+        bank = transpose_unit(base_unit((2, 3)))
+        g_b1 = regroup_unit(sca, bank, "b1")
+        b1 = quantise_unit(g_b1, "b1")
+        bank = transpose_unit(spline_unit(4))
+        g_s4 = regroup_unit(sca, bank, "s4")
+        bank = transpose_unit(spline_unit(5))
+        g_s5 = regroup_unit(sca, bank, "s5")
+        acc01 = multiply_pair(s0, s1, b0)
+        bank4 = transpose_unit(base_unit((4,)))
+        bank5 = transpose_unit(base_unit((5,)))
+        s4 = quantise_unit(g_s4, "s4")
+        g_b5 = regroup_unit(vec, bank5, "b5")
+        g_b4 = regroup_unit(sca, bank4, "b4")
+        s5 = quantise_unit(g_s5, "s5")
+        b5 = quantise_unit(g_b5, "b5")
+        b4 = quantise_unit(g_b4, "b4")
+        acc23 = multiply_pair(s2, s3, b1)
+        store(sca, acc01, 0)
+        store(sca, acc23, 2 * P)
+        acc4 = sums.tile([P, P], F32, tag="acc", name="acc4")
+        acc5 = sums.tile([P, P], F32, tag="acc", name="acc5")
+        for c in range(SPLINE_PASSES):
+            multiply(acc4[:], c, s4, c)
+        for c in range(SPLINE_PASSES):
+            multiply(acc5[:], c, s5, c)
+        multiply(acc5[:], SPLINE_PASSES, b5, 0)
+        multiply(acc4[:], SPLINE_PASSES, b4, 0)
+        store(vec, acc5, 5 * P)
+        store(sca, acc4, 4 * P)

@@ -18,8 +18,9 @@ PACK = 4
 HALVES = 2
 SPLINE_PASSES = 2
 PASSES = 3
-TILES = OUTPUTS // P
-PAIRS = TILES // 2
+GROUP = 256
+GROUPS = OUTPUTS // GROUP
+ROWS = GROUP // P
 CENTRES = (-1.0, 1.0)
 HAT_SLOPE = 0.5
 
@@ -41,23 +42,17 @@ def tile_generatorhead_pb_s_kernel(tc, h_norm, base_w2, spline_w2, out):
 
         x_rows = loaded.tile([P, FEATURES], BF16, name="x_rows")
         nc.sync.dma_start(out=x_rows[:], in_=x_dram)
-        spline_rows = {}
-        base_rows = {}
-        for q in range(PAIRS):
-            for j in (2 * q, 2 * q + 1):
-                rows = loaded.tile([P, FEATURES * BASES], BF16, name="spline_rows%d" % j)
-                nc.sync.dma_start(out=rows[:], in_=spline_w2[j * P : (j + 1) * P, :, :].rearrange("p i c -> p (i c)"))
-                spline_rows[j] = rows
-            if q < PAIRS - 1:
-                rows = loaded.tile([P, 2, FEATURES], BF16, name="base_rows%d" % q)
-                nc.sync.dma_start(out=rows[:], in_=base_w2[2 * q * P : (2 * q + 2) * P, :].rearrange("(r p) i -> p r i", p=P))
-                base_rows[2 * q] = rows[:, 0, :]
-                base_rows[2 * q + 1] = rows[:, 1, :]
-            else:
-                for j in (2 * q, 2 * q + 1):
-                    rows = loaded.tile([P, FEATURES], BF16, name="base_rows_tile%d" % j)
-                    nc.sync.dma_start(out=rows[:], in_=base_w2[j * P : (j + 1) * P, :])
-                    base_rows[j] = rows[:]
+        spline_rows = []
+        base_rows = []
+        for g in range(GROUPS):
+            outputs = slice(g * GROUP, (g + 1) * GROUP)
+            rows = loaded.tile([P, ROWS, FEATURES * BASES], BF16, name="spline_rows%d" % g)
+            nc.sync.dma_start(out=rows[:], in_=spline_w2[outputs, :, :].rearrange("(p r) i c -> p r (i c)", r=ROWS))
+            spline_rows.append(rows)
+            rows = loaded.tile([P, ROWS, FEATURES], BF16, name="base_rows%d" % g)
+            order = "(p r) i -> p r i" if g < GROUPS - 1 else "(r p) i -> p r i"
+            nc.sync.dma_start(out=rows[:], in_=base_w2[outputs, :].rearrange(order, r=ROWS))
+            base_rows.append(rows)
 
         ident_f32 = consts.tile([P, P], F32, name="ident_f32")
         make_identity(nc, ident_f32[:])
@@ -98,58 +93,52 @@ def tile_generatorhead_pb_s_kernel(tc, h_norm, base_w2, spline_w2, out):
             nc.vector.quantize_mx(out=x_codes[:, spline_cols].bitcast(FP8X4), scales=x_scales[:, spline_cols], in_=hats_grouped[:])
             nc.vector.quantize_mx(out=x_codes[:, base_cols].bitcast(FP8X4), scales=x_scales[:, base_cols], in_=silu_grouped[:])
 
-        def spline_unit(j):
-            words = spline_rows[j][:].bitcast(F32).rearrange("p (s k h) -> p s h k", k=P, h=HALVES)
-            return [words[:, s, :, :] for s in range(SPLINE_PASSES)]
+        def spline_words(g, s):
+            return spline_rows[g][:].rearrange("p r n -> p (r n)").bitcast(F32).rearrange("p (r s k h) -> p r s h k", r=ROWS, k=P, h=HALVES)[:, :, s, :, :]
 
-        def base_unit(tiles):
-            return [base_rows[j].bitcast(F32).rearrange("p (h k) -> p h k", h=HALVES) for j in tiles]
+        def base_words(g):
+            return base_rows[g][:].rearrange("p r n -> p (r n)").bitcast(F32).rearrange("p (r h k) -> p r h k", r=ROWS, h=HALVES)
 
-        def transpose_unit(blocks):
-            bank = banks.tile([P, len(blocks) * HALVES, P], F32, tag="bank", name="bank")
-            for b in range(len(blocks)):
+        def transpose_rows(words, rows):
+            bank = banks.tile([P, len(rows) * HALVES, P], F32, tag="bank", name="bank")
+            for r in range(len(rows)):
                 for h in range(HALVES):
-                    nc.tensor.transpose(bank[:, b * HALVES + h, :], blocks[b][:, h, :], ident_f32[:])
+                    nc.tensor.transpose(bank[:, r * HALVES + h, :], words[:, rows[r], h, :], ident_f32[:])
             return bank
 
-        def regroup_unit(copy_out, bank, name):
-            n = bank.shape[1] // HALVES
-            grouped = keep.tile([P, n * P * PACK], BF16, name="grouped_" + name, align_bytes=64)
+        def regroup(copy_out, bank, name):
+            n = bank.shape[1]
+            grouped = keep.tile([P, n * P * 2], BF16, name="grouped_" + name, align_bytes=64)
             copy_out(
-                out=grouped[:].bitcast(F32).rearrange("k (b p h) -> k b p h", b=n, h=HALVES),
-                in_=bank[:].rearrange("k (b h) p -> k b p h", h=HALVES),
+                out=grouped[:].bitcast(F32).rearrange("k (p h) -> k p h", h=n),
+                in_=bank[:].rearrange("k h p -> k p h"),
             )
             return grouped
 
-        def quantise_unit(grouped, name):
+        def quantise(grouped, name):
             n = grouped.shape[1] // PACK
             codes = keep.tile([P, n], U32, name="codes_" + name, align_bytes=64)
             scales = keep.tile([P, n], U8, name="scales_" + name, align_bytes=64)
             nc.vector.quantize_mx(out=codes[:].bitcast(FP8X4), scales=scales[:], in_=grouped[:])
             return codes, scales
 
-        def multiply(acc_cols, c, operand, b):
+        def multiply(acc, c, operand, first=0):
             codes, scales = operand
+            cols = slice(first, first + acc.shape[1])
             nc.tensor.matmul_mx(
-                out=acc_cols,
+                out=acc[:],
                 lhsT=x_codes[:, c * P : (c + 1) * P].bitcast(FP8X4),
                 lhsT_scale=x_scales[:, c * P : (c + 1) * P],
-                rhs=codes[:, b * P : (b + 1) * P].bitcast(FP8X4),
-                rhs_scale=scales[:, b * P : (b + 1) * P],
+                rhs=codes[:, cols].bitcast(FP8X4),
+                rhs_scale=scales[:, cols],
                 start=(c == 0),
                 stop=(c == PASSES - 1),
             )
 
-        vec = nc.vector.tensor_copy
-        sca = nc.scalar.copy
-
-        def multiply_pair(s_even, s_odd, b_both):
-            acc = sums.tile([P, 2 * P], F32, tag="acc", name="acc")
-            for r in range(2):
-                cols = acc[:, r * P : (r + 1) * P]
-                multiply(cols, 0, (s_even, s_odd)[r], 0)
-                multiply(cols, 1, (s_even, s_odd)[r], 1)
-                multiply(cols, 2, b_both, r)
+        def multiply_group(operands):
+            acc = sums.tile([P, GROUP], F32, tag="acc", name="acc")
+            for c in range(PASSES):
+                multiply(acc, c, operands[c])
             return acc
 
         def store(copy_out, acc, first):
@@ -158,48 +147,44 @@ def tile_generatorhead_pb_s_kernel(tc, h_norm, base_w2, spline_w2, out):
             copy_out(out=result[:], in_=acc[:])
             nc.sync.dma_start(out=out_dram[:, first : first + width], in_=result[:])
 
-        bank = transpose_unit(spline_unit(0))
-        g_s0 = regroup_unit(vec, bank, "s0")
-        bank = transpose_unit(spline_unit(1))
-        g_s1 = regroup_unit(vec, bank, "s1")
-        s0 = quantise_unit(g_s0, "s0")
-        bank = transpose_unit(base_unit((0, 1)))
-        g_b0 = regroup_unit(vec, bank, "b0")
-        s1 = quantise_unit(g_s1, "s1")
-        b0 = quantise_unit(g_b0, "b0")
+        vec = nc.vector.tensor_copy
+        sca = nc.scalar.copy
+        both = (0, 1)
+
+        g00 = regroup(vec, transpose_rows(spline_words(0, 0), both), "00")
+        g01 = regroup(vec, transpose_rows(spline_words(0, 1), both), "01")
+        q00 = quantise(g00, "00")
+        g02 = regroup(vec, transpose_rows(base_words(0), both), "02")
+        q01 = quantise(g01, "01")
+        q02 = quantise(g02, "02")
         quantise_x()
-        bank = transpose_unit(spline_unit(2))
-        g_s2 = regroup_unit(sca, bank, "s2")
-        s2 = quantise_unit(g_s2, "s2")
-        bank = transpose_unit(spline_unit(3))
-        g_s3 = regroup_unit(sca, bank, "s3")
-        s3 = quantise_unit(g_s3, "s3")
-        bank = transpose_unit(base_unit((2, 3)))
-        g_b1 = regroup_unit(sca, bank, "b1")
-        b1 = quantise_unit(g_b1, "b1")
-        bank = transpose_unit(spline_unit(4))
-        g_s4 = regroup_unit(sca, bank, "s4")
-        bank = transpose_unit(spline_unit(5))
-        g_s5 = regroup_unit(sca, bank, "s5")
-        acc01 = multiply_pair(s0, s1, b0)
-        bank4 = transpose_unit(base_unit((4,)))
-        bank5 = transpose_unit(base_unit((5,)))
-        s4 = quantise_unit(g_s4, "s4")
-        g_b5 = regroup_unit(vec, bank5, "b5")
-        g_b4 = regroup_unit(sca, bank4, "b4")
-        s5 = quantise_unit(g_s5, "s5")
-        b5 = quantise_unit(g_b5, "b5")
-        b4 = quantise_unit(g_b4, "b4")
-        acc23 = multiply_pair(s2, s3, b1)
-        store(sca, acc01, 0)
-        store(sca, acc23, 2 * P)
-        acc4 = sums.tile([P, P], F32, tag="acc", name="acc4")
-        acc5 = sums.tile([P, P], F32, tag="acc", name="acc5")
-        for c in range(SPLINE_PASSES):
-            multiply(acc4[:], c, s4, c)
-        for c in range(SPLINE_PASSES):
-            multiply(acc5[:], c, s5, c)
-        multiply(acc5[:], SPLINE_PASSES, b5, 0)
-        multiply(acc4[:], SPLINE_PASSES, b4, 0)
-        store(vec, acc5, 5 * P)
-        store(sca, acc4, 4 * P)
+        g10 = regroup(sca, transpose_rows(spline_words(1, 0), both), "10")
+        g11 = regroup(sca, transpose_rows(spline_words(1, 1), both), "11")
+        q10 = quantise(g10, "10")
+        g12 = regroup(vec, transpose_rows(base_words(1), both), "12")
+        q11 = quantise(g11, "11")
+        q12 = quantise(g12, "12")
+        g20 = regroup(sca, transpose_rows(spline_words(2, 0), both), "20")
+        g21 = regroup(sca, transpose_rows(spline_words(2, 1), both), "21")
+        q20 = quantise(g20, "20")
+        acc0 = multiply_group((q00, q01, q02))
+        bank_a = transpose_rows(base_words(2), (0,))
+        bank_b = transpose_rows(base_words(2), (1,))
+        g22b = regroup(vec, bank_b, "22b")
+        g22a = regroup(sca, bank_a, "22a")
+        q21 = quantise(g21, "21")
+        q22b = quantise(g22b, "22b")
+        q22a = quantise(g22a, "22a")
+        acc1 = multiply_group((q10, q11, q12))
+        store(sca, acc0, 0)
+        store(sca, acc1, GROUP)
+        acc_a = sums.tile([P, P], F32, tag="acc", name="acc_a")
+        acc_b = sums.tile([P, P], F32, tag="acc", name="acc_b")
+        multiply(acc_a, 0, q20, 0)
+        multiply(acc_b, 0, q20, P)
+        multiply(acc_a, 1, q21, 0)
+        multiply(acc_b, 1, q21, P)
+        multiply(acc_b, 2, q22b)
+        multiply(acc_a, 2, q22a)
+        store(vec, acc_b, 2 * GROUP + P)
+        store(sca, acc_a, 2 * GROUP)

@@ -167,7 +167,6 @@ def tile_generatorhead_pb_s_kernel(tc, h_norm, base_w2, spline_w2, out):
         g20 = regroup(sca, transpose_rows(spline_words(2, 0), both), "20")
         g21 = regroup(sca, transpose_rows(spline_words(2, 1), both), "21")
         q20 = quantise(g20, "20")
-        acc0 = multiply_group((q00, q01, q02))
         bank_a = transpose_rows(base_words(2), (0,))
         bank_b = transpose_rows(base_words(2), (1,))
         g22b = regroup(vec, bank_b, "22b")
@@ -175,6 +174,7 @@ def tile_generatorhead_pb_s_kernel(tc, h_norm, base_w2, spline_w2, out):
         q21 = quantise(g21, "21")
         q22b = quantise(g22b, "22b")
         q22a = quantise(g22a, "22a")
+        acc0 = multiply_group((q00, q01, q02))
         acc1 = multiply_group((q10, q11, q12))
         store(sca, acc0, 0)
         store(sca, acc1, GROUP)

@@ -186,5 +186,7 @@ def tile_generatorhead_pb_s_kernel(tc, h_norm, base_w2, spline_w2, out):
         multiply(acc_b, 1, q21, P)
         multiply(acc_b, 2, q22b)
         multiply(acc_a, 2, q22a)
-        store(vec, acc_b, 2 * GROUP + P)
-        store(sca, acc_a, 2 * GROUP)
+        last = keep.tile([P, GROUP], F32, name="result_last")
+        nc.vector.tensor_copy(out=last[:, P:], in_=acc_b[:])
+        nc.scalar.copy(out=last[:, :P], in_=acc_a[:])
+        nc.sync.dma_start(out=out_dram[:, 2 * GROUP :], in_=last[:])

@@ -36,8 +36,7 @@ def tile_generatorhead_pb_s_kernel(tc, h_norm, base_w2, spline_w2, out):
         consts = ctx.enter_context(tc.tile_pool(name="consts", bufs=1))
         loaded = ctx.enter_context(tc.tile_pool(name="loaded", bufs=1))
         keep = ctx.enter_context(tc.tile_pool(name="keep", bufs=1))
-        banks = ctx.enter_context(tc.psum_pool(name="banks", bufs=4))
-        sums = ctx.enter_context(tc.psum_pool(name="sums", bufs=4))
+        banks = ctx.enter_context(tc.psum_pool(name="banks", bufs=8))
         ctx.enter_context(tc.manual_schedule())
 
         x_rows = loaded.tile([P, FEATURES], BF16, name="x_rows")
@@ -50,8 +49,7 @@ def tile_generatorhead_pb_s_kernel(tc, h_norm, base_w2, spline_w2, out):
             nc.sync.dma_start(out=rows[:], in_=spline_w2[outputs, :, :].rearrange("(p r) i c -> p r (i c)", r=ROWS))
             spline_rows.append(rows)
             rows = loaded.tile([P, ROWS, FEATURES], BF16, name="base_rows%d" % g)
-            order = "(p r) i -> p r i" if g < GROUPS - 1 else "(r p) i -> p r i"
-            nc.sync.dma_start(out=rows[:], in_=base_w2[outputs, :].rearrange(order, r=ROWS))
+            nc.sync.dma_start(out=rows[:], in_=base_w2[outputs, :].rearrange("(p r) i -> p r i", r=ROWS))
             base_rows.append(rows)
 
         ident_f32 = consts.tile([P, P], F32, name="ident_f32")
@@ -136,7 +134,7 @@ def tile_generatorhead_pb_s_kernel(tc, h_norm, base_w2, spline_w2, out):
             )
 
         def multiply_group(operands):
-            acc = sums.tile([P, GROUP], F32, tag="acc", name="acc")
+            acc = banks.tile([P, GROUP], F32, tag="bank", name="acc")
             for c in range(PASSES):
                 multiply(acc, c, operands[c])
             return acc
@@ -161,32 +159,18 @@ def tile_generatorhead_pb_s_kernel(tc, h_norm, base_w2, spline_w2, out):
         g10 = regroup(sca, transpose_rows(spline_words(1, 0), both), "10")
         g11 = regroup(sca, transpose_rows(spline_words(1, 1), both), "11")
         q10 = quantise(g10, "10")
-        g12 = regroup(vec, transpose_rows(base_words(1), both), "12")
+        g12 = regroup(sca, transpose_rows(base_words(1), both), "12")
         q11 = quantise(g11, "11")
+        bank20 = transpose_rows(spline_words(2, 0), both)
+        bank21 = transpose_rows(spline_words(2, 1), both)
+        bank22 = transpose_rows(base_words(2), both)
+        g20 = regroup(sca, bank20, "20")
+        g21 = regroup(vec, bank21, "21")
         q12 = quantise(g12, "12")
-        g20 = regroup(sca, transpose_rows(spline_words(2, 0), both), "20")
-        g21 = regroup(sca, transpose_rows(spline_words(2, 1), both), "21")
+        g22 = regroup(sca, bank22, "22")
         q20 = quantise(g20, "20")
-        bank_a = transpose_rows(base_words(2), (0,))
-        bank_b = transpose_rows(base_words(2), (1,))
-        g22b = regroup(vec, bank_b, "22b")
-        g22a = regroup(sca, bank_a, "22a")
         q21 = quantise(g21, "21")
-        q22b = quantise(g22b, "22b")
-        q22a = quantise(g22a, "22a")
-        acc0 = multiply_group((q00, q01, q02))
-        acc1 = multiply_group((q10, q11, q12))
-        store(sca, acc0, 0)
-        store(sca, acc1, GROUP)
-        acc_a = sums.tile([P, P], F32, tag="acc", name="acc_a")
-        acc_b = sums.tile([P, P], F32, tag="acc", name="acc_b")
-        multiply(acc_a, 0, q20, 0)
-        multiply(acc_b, 0, q20, P)
-        multiply(acc_a, 1, q21, 0)
-        multiply(acc_b, 1, q21, P)
-        multiply(acc_b, 2, q22b)
-        multiply(acc_a, 2, q22a)
-        last = keep.tile([P, GROUP], F32, name="result_last")
-        nc.vector.tensor_copy(out=last[:, P:], in_=acc_b[:])
-        nc.scalar.copy(out=last[:, :P], in_=acc_a[:])
-        nc.sync.dma_start(out=out_dram[:, 2 * GROUP :], in_=last[:])
+        q22 = quantise(g22, "22")
+        store(sca, multiply_group((q00, q01, q02)), 0)
+        store(vec, multiply_group((q10, q11, q12)), GROUP)
+        store(sca, multiply_group((q20, q21, q22)), 2 * GROUP)

@@ -21,6 +21,7 @@ PASSES = 3
 GROUP = 256
 GROUPS = OUTPUTS // GROUP
 ROWS = GROUP // P
+WARM_UP = 8
 CENTRES = (-1.0, 1.0)
 HAT_SLOPE = 0.5
 
@@ -54,15 +55,43 @@ def tile_generatorhead_pb_s_kernel(tc, h_norm, base_w2, spline_w2, out):
 
         ident_f32 = consts.tile([P, P], F32, name="ident_f32")
         make_identity(nc, ident_f32[:])
+        ident_bf16 = consts.tile([P, P], BF16, name="ident_bf16")
+        make_identity(nc, ident_bf16[:])
+
+        def quantise(grouped, name):
+            n = grouped.shape[1] // PACK
+            codes = keep.tile([P, n], U32, name="codes_" + name, align_bytes=64)
+            scales = keep.tile([P, n], U8, name="scales_" + name, align_bytes=64)
+            nc.vector.quantize_mx(out=codes[:].bitcast(FP8X4), scales=scales[:], in_=grouped[:])
+            return codes, scales
+
+        zeros = consts.tile([P, P * PACK], BF16, name="zeros", align_bytes=64)
+        nc.vector.memset(zeros[:].bitcast(U32), 0)
+        zero_codes, zero_scales = quantise(zeros, "zeros")
         minus_centre = consts.tile([P, BASES], F32, name="minus_centre")
         for c in range(BASES):
             nc.vector.memset(minus_centre[:, c : c + 1], -CENTRES[c])
         one = consts.tile([P, 1], F32, name="one")
         nc.vector.memset(one[:], 1.0)
+        idle_bank = banks.tile([P, P], F32, tag="bank", name="idle_bank")
+        for n in range(WARM_UP):
+            nc.tensor.matmul_mx(
+                out=idle_bank[:],
+                lhsT=zero_codes[:].bitcast(FP8X4),
+                lhsT_scale=zero_scales[:],
+                rhs=zero_codes[:].bitcast(FP8X4),
+                rhs_scale=zero_scales[:],
+                start=True,
+                stop=True,
+            )
 
         x_words = banks.tile([P, HALVES * P], F32, tag="bank", name="x_words")
         for u in range(HALVES):
             nc.tensor.transpose(x_words[:, u * P : (u + 1) * P], x_rows[:].bitcast(F32)[:, u * P : (u + 1) * P], ident_f32[:])
+
+        x_feats = banks.tile([P, SPLINE_PASSES * HALVES, P], BF16, tag="bank", name="x_feats")
+        for f in range(SPLINE_PASSES * HALVES):
+            nc.tensor.transpose(x_feats[:, f, :], x_rows[:, f * P : (f + 1) * P], ident_bf16[:])
 
         silu_grouped = keep.tile([P, P * PACK], BF16, name="silu_grouped", align_bytes=64)
         nc.scalar.activation(
@@ -72,7 +101,12 @@ def tile_generatorhead_pb_s_kernel(tc, h_norm, base_w2, spline_w2, out):
         )
         distance = keep.tile([P, BASES, FEATURES], F32, name="distance")
         for c in range(BASES):
-            nc.scalar.activation(out=distance[:, c, :], in_=x_words[:].bitcast(BF16), func=ACT.Abs, bias=minus_centre[:, c : c + 1])
+            nc.scalar.activation(
+                out=distance[:, c, :].rearrange("p (s t h) -> p s t h", s=SPLINE_PASSES, h=HALVES),
+                in_=x_feats[:].rearrange("p (s h) t -> p s t h", h=HALVES),
+                func=ACT.Abs,
+                bias=minus_centre[:, c : c + 1],
+            )
         hats_grouped = keep.tile([P, FEATURES * BASES], BF16, name="hats_grouped", align_bytes=64)
         nc.scalar.activation(
             out=hats_grouped[:].rearrange("p (n c) -> p n c", c=BASES),
@@ -92,7 +126,7 @@ def tile_generatorhead_pb_s_kernel(tc, h_norm, base_w2, spline_w2, out):
             nc.vector.quantize_mx(out=x_codes[:, base_cols].bitcast(FP8X4), scales=x_scales[:, base_cols], in_=silu_grouped[:])
 
         def spline_words(g, s):
-            return spline_rows[g][:].rearrange("p r n -> p (r n)").bitcast(F32).rearrange("p (r s k h) -> p r s h k", r=ROWS, k=P, h=HALVES)[:, :, s, :, :]
+            return spline_rows[g][:].rearrange("p r n -> p (r n)").bitcast(F32).rearrange("p (r s h k) -> p r s h k", r=ROWS, k=P, h=HALVES)[:, :, s, :, :]
 
         def base_words(g):
             return base_rows[g][:].rearrange("p r n -> p (r n)").bitcast(F32).rearrange("p (r h k) -> p r h k", r=ROWS, h=HALVES)
@@ -112,13 +146,6 @@ def tile_generatorhead_pb_s_kernel(tc, h_norm, base_w2, spline_w2, out):
                 in_=bank[:].rearrange("k h p -> k p h"),
             )
             return grouped
-
-        def quantise(grouped, name):
-            n = grouped.shape[1] // PACK
-            codes = keep.tile([P, n], U32, name="codes_" + name, align_bytes=64)
-            scales = keep.tile([P, n], U8, name="scales_" + name, align_bytes=64)
-            nc.vector.quantize_mx(out=codes[:].bitcast(FP8X4), scales=scales[:], in_=grouped[:])
-            return codes, scales
 
         def multiply(acc, c, operand, first=0):
             codes, scales = operand

@@ -9,6 +9,7 @@ U32 = mybir.dt.uint32
 U8 = mybir.dt.uint8
 FP8X4 = mybir.dt.float8_e4m3fn_x4
 ACT = mybir.ActivationFunctionType
+ALU = mybir.AluOpType
 
 P = 128
 FEATURES = 512
@@ -42,16 +43,29 @@ def tile_generatorhead_pb_s_kernel(tc, h_norm, base_w2, spline_w2, out):
 
         x_rows = loaded.tile([P, FEATURES], BF16, name="x_rows")
         nc.sync.dma_start(out=x_rows[:], in_=x_dram)
-        spline_rows = []
-        base_rows = []
-        for g in range(GROUPS):
-            outputs = slice(g * GROUP, (g + 1) * GROUP)
-            rows = loaded.tile([P, ROWS, FEATURES * BASES], BF16, name="spline_rows%d" % g)
-            nc.sync.dma_start(out=rows[:], in_=spline_w2[outputs, :, :].rearrange("(p r) i c -> p r (i c)", r=ROWS))
-            spline_rows.append(rows)
-            rows = loaded.tile([P, ROWS, FEATURES], BF16, name="base_rows%d" % g)
-            nc.sync.dma_start(out=rows[:], in_=base_w2[outputs, :].rearrange("(p r) i -> p r i", r=ROWS))
-            base_rows.append(rows)
+        spline_rows = [loaded.tile([P, ROWS, FEATURES * BASES], BF16, name="spline_rows%d" % g) for g in range(GROUPS)]
+        base_rows = [loaded.tile([P, ROWS, FEATURES], BF16, name="base_rows%d" % g) for g in range(GROUPS)]
+
+        def load_spline(g, rows):
+            source = spline_w2[g * GROUP : (g + 1) * GROUP, :, :].rearrange("(p r) i c -> p r (i c)", r=ROWS)
+            nc.sync.dma_start(out=spline_rows[g][:, rows, :], in_=source[:, rows, :])
+
+        def load_base(g):
+            source = base_w2[g * GROUP : (g + 1) * GROUP, :].rearrange("(p r) i -> p r i", r=ROWS)
+            nc.sync.dma_start(out=base_rows[g][:], in_=source)
+
+        def load_last_base(r):
+            first = (GROUPS - 1) * GROUP + r * P
+            nc.sync.dma_start(out=base_rows[GROUPS - 1][:, r, :], in_=base_w2[first : first + P, :])
+
+        load_base(0)
+        load_spline(0, slice(0, ROWS))
+        load_spline(1, slice(0, ROWS))
+        load_base(1)
+        for r in range(ROWS):
+            load_spline(2, slice(r, r + 1))
+        for r in range(ROWS):
+            load_last_base(r)
 
         ident_f32 = consts.tile([P, P], F32, name="ident_f32")
         make_identity(nc, ident_f32[:])
@@ -62,17 +76,15 @@ def tile_generatorhead_pb_s_kernel(tc, h_norm, base_w2, spline_w2, out):
             n = grouped.shape[1] // PACK
             codes = keep.tile([P, n], U32, name="codes_" + name, align_bytes=64)
             scales = keep.tile([P, n], U8, name="scales_" + name, align_bytes=64)
-            nc.vector.quantize_mx(out=codes[:].bitcast(FP8X4), scales=scales[:], in_=grouped[:])
+            nc.vector.quantize_mx(out=codes[:].bitcast(FP8X4), scales=scales[:], in_=grouped)
             return codes, scales
 
         zeros = consts.tile([P, P * PACK], BF16, name="zeros", align_bytes=64)
         nc.vector.memset(zeros[:].bitcast(U32), 0)
-        zero_codes, zero_scales = quantise(zeros, "zeros")
+        zero_codes, zero_scales = quantise(zeros[:], "zeros")
         minus_centre = consts.tile([P, BASES], F32, name="minus_centre")
         for c in range(BASES):
-            nc.vector.memset(minus_centre[:, c : c + 1], -CENTRES[c])
-        one = consts.tile([P, 1], F32, name="one")
-        nc.vector.memset(one[:], 1.0)
+            nc.vector.memset(minus_centre[:, c : c + 1], -HAT_SLOPE * CENTRES[c])
         idle_bank = banks.tile([P, P], F32, tag="bank", name="idle_bank")
         for n in range(WARM_UP):
             nc.tensor.matmul_mx(
@@ -105,25 +117,35 @@ def tile_generatorhead_pb_s_kernel(tc, h_norm, base_w2, spline_w2, out):
                 out=distance[:, c, :].rearrange("p (s t h) -> p s t h", s=SPLINE_PASSES, h=HALVES),
                 in_=x_feats[:].rearrange("p (s h) t -> p s t h", h=HALVES),
                 func=ACT.Abs,
+                scale=HAT_SLOPE,
                 bias=minus_centre[:, c : c + 1],
             )
-        hats_grouped = keep.tile([P, FEATURES * BASES], BF16, name="hats_grouped", align_bytes=64)
-        nc.scalar.activation(
-            out=hats_grouped[:].rearrange("p (n c) -> p n c", c=BASES),
-            in_=distance[:].rearrange("p c n -> p n c"),
-            func=ACT.Relu,
-            scale=-HAT_SLOPE,
-            bias=one[:],
-        )
+        minus_silu = keep.tile([P, P * PACK], BF16, name="minus_silu", align_bytes=64)
+        minus_hats = keep.tile([P, FEATURES * BASES], BF16, name="minus_hats", align_bytes=64)
+
+        def negate_silu():
+            nc.vector.tensor_scalar_mul(out=minus_silu[:], in0=silu_grouped[:], scalar1=-1.0)
+
+        def finish_hats():
+            nc.vector.tensor_scalar(
+                out=minus_hats[:].rearrange("p (n c) -> p n c", c=BASES),
+                in0=distance[:].rearrange("p c n -> p n c"),
+                scalar1=1.0,
+                scalar2=1.0,
+                op0=ALU.min,
+                op1=ALU.subtract,
+            )
 
         x_codes = keep.tile([P, PASSES * P], U32, name="x_codes", align_bytes=64)
         x_scales = keep.tile([P, PASSES * P], U8, name="x_scales", align_bytes=64)
 
-        def quantise_x():
-            spline_cols = slice(0, SPLINE_PASSES * P)
-            base_cols = slice(SPLINE_PASSES * P, PASSES * P)
-            nc.vector.quantize_mx(out=x_codes[:, spline_cols].bitcast(FP8X4), scales=x_scales[:, spline_cols], in_=hats_grouped[:])
-            nc.vector.quantize_mx(out=x_codes[:, base_cols].bitcast(FP8X4), scales=x_scales[:, base_cols], in_=silu_grouped[:])
+        def quantise_hats():
+            cols = slice(0, SPLINE_PASSES * P)
+            nc.vector.quantize_mx(out=x_codes[:, cols].bitcast(FP8X4), scales=x_scales[:, cols], in_=minus_hats[:])
+
+        def quantise_silu():
+            cols = slice(SPLINE_PASSES * P, PASSES * P)
+            nc.vector.quantize_mx(out=x_codes[:, cols].bitcast(FP8X4), scales=x_scales[:, cols], in_=minus_silu[:])
 
         def spline_words(g, s):
             return spline_rows[g][:].rearrange("p r n -> p (r n)").bitcast(F32).rearrange("p (r s h k) -> p r s h k", r=ROWS, k=P, h=HALVES)[:, :, s, :, :]
@@ -131,11 +153,17 @@ def tile_generatorhead_pb_s_kernel(tc, h_norm, base_w2, spline_w2, out):
         def base_words(g):
             return base_rows[g][:].rearrange("p r n -> p (r n)").bitcast(F32).rearrange("p (r h k) -> p r h k", r=ROWS, h=HALVES)
 
-        def transpose_rows(words, rows):
-            bank = banks.tile([P, len(rows) * HALVES, P], F32, tag="bank", name="bank")
-            for r in range(len(rows)):
-                for h in range(HALVES):
-                    nc.tensor.transpose(bank[:, r * HALVES + h, :], words[:, rows[r], h, :], ident_f32[:])
+        def new_bank(rows):
+            return banks.tile([P, rows * HALVES, P], F32, tag="bank", name="bank")
+
+        def transpose_row(bank, b, words, r):
+            for h in range(HALVES):
+                nc.tensor.transpose(bank[:, b * HALVES + h, :], words[:, r, h, :], ident_f32[:])
+
+        def transpose_rows(words):
+            bank = new_bank(ROWS)
+            for r in range(ROWS):
+                transpose_row(bank, r, words, r)
             return bank
 
         def regroup(copy_out, bank, name):
@@ -145,7 +173,7 @@ def tile_generatorhead_pb_s_kernel(tc, h_norm, base_w2, spline_w2, out):
                 out=grouped[:].bitcast(F32).rearrange("k (p h) -> k p h", h=n),
                 in_=bank[:].rearrange("k h p -> k p h"),
             )
-            return grouped
+            return grouped[:]
 
         def multiply(acc, c, operand, first=0):
             codes, scales = operand
@@ -166,38 +194,50 @@ def tile_generatorhead_pb_s_kernel(tc, h_norm, base_w2, spline_w2, out):
                 multiply(acc, c, operands[c])
             return acc
 
-        def store(copy_out, acc, first):
-            width = acc.shape[1]
-            result = keep.tile([P, width], F32, name="result%d" % first)
-            copy_out(out=result[:], in_=acc[:])
-            nc.sync.dma_start(out=out_dram[:, first : first + width], in_=result[:])
+        def store(acc, g):
+            result = keep.tile([P, GROUP], F32, name="result%d" % g)
+            nc.scalar.activation(out=result[:], in_=acc[:], func=ACT.Copy, scale=-1.0)
+            nc.sync.dma_start(out=out_dram[:, g * GROUP : (g + 1) * GROUP], in_=result[:])
 
         vec = nc.vector.tensor_copy
         sca = nc.scalar.copy
-        both = (0, 1)
-
-        g00 = regroup(vec, transpose_rows(spline_words(0, 0), both), "00")
-        g01 = regroup(vec, transpose_rows(spline_words(0, 1), both), "01")
-        q00 = quantise(g00, "00")
-        g02 = regroup(vec, transpose_rows(base_words(0), both), "02")
-        q01 = quantise(g01, "01")
+        negate_silu()
+        g02 = regroup(vec, transpose_rows(base_words(0)), "02")
+        quantise_silu()
         q02 = quantise(g02, "02")
-        quantise_x()
-        g10 = regroup(sca, transpose_rows(spline_words(1, 0), both), "10")
-        g11 = regroup(sca, transpose_rows(spline_words(1, 1), both), "11")
+        finish_hats()
+        g00 = regroup(sca, transpose_rows(spline_words(0, 0)), "00")
+        g01 = regroup(sca, transpose_rows(spline_words(0, 1)), "01")
+        q00 = quantise(g00, "00")
+        q01 = quantise(g01, "01")
+        quantise_hats()
+        g10 = regroup(sca, transpose_rows(spline_words(1, 0)), "10")
+        g11 = regroup(vec, transpose_rows(spline_words(1, 1)), "11")
+        g12 = regroup(sca, transpose_rows(base_words(1)), "12")
         q10 = quantise(g10, "10")
-        g12 = regroup(sca, transpose_rows(base_words(1), both), "12")
         q11 = quantise(g11, "11")
-        bank20 = transpose_rows(spline_words(2, 0), both)
-        bank21 = transpose_rows(spline_words(2, 1), both)
-        bank22 = transpose_rows(base_words(2), both)
-        g20 = regroup(sca, bank20, "20")
-        g21 = regroup(vec, bank21, "21")
         q12 = quantise(g12, "12")
-        g22 = regroup(sca, bank22, "22")
+        spline_banks = [new_bank(ROWS) for c in range(SPLINE_PASSES)]
+        for r in range(ROWS):
+            for c in range(SPLINE_PASSES):
+                transpose_row(spline_banks[c], r, spline_words(2, c), r)
+        base_banks = [new_bank(1) for r in range(ROWS)]
+        for r in range(ROWS):
+            transpose_row(base_banks[r], 0, base_words(2), r)
+        g20 = regroup(sca, spline_banks[0], "20")
+        g21 = regroup(sca, spline_banks[1], "21")
         q20 = quantise(g20, "20")
         q21 = quantise(g21, "21")
-        q22 = quantise(g22, "22")
-        store(sca, multiply_group((q00, q01, q02)), 0)
-        store(vec, multiply_group((q10, q11, q12)), GROUP)
-        store(sca, multiply_group((q20, q21, q22)), 2 * GROUP)
+        q22 = [quantise(regroup(sca, base_banks[r], "22_%d" % r), "22_%d" % r) for r in range(ROWS)]
+        store(multiply_group((q00, q01, q02)), 0)
+        store(multiply_group((q10, q11, q12)), 1)
+        halves = [banks.tile([P, P], F32, tag="bank", name="half%d" % r) for r in range(ROWS)]
+        for r in range(ROWS):
+            multiply(halves[r], 0, q20, r * P)
+            multiply(halves[r], 1, q21, r * P)
+        for r in range(ROWS):
+            multiply(halves[r], 2, q22[r])
+        last = keep.tile([P, GROUP], F32, name="result_last")
+        nc.scalar.activation(out=last[:, :P], in_=halves[0][:], func=ACT.Copy, scale=-1.0)
+        nc.vector.tensor_scalar_mul(out=last[:, P:], in0=halves[1][:], scalar1=-1.0)
+        nc.sync.dma_start(out=out_dram[:, 2 * GROUP :], in_=last[:])

from contextlib import ExitStack

import concourse.mybir as mybir
from concourse.masks import make_identity

BF16 = mybir.dt.bfloat16
F32 = mybir.dt.float32
U32 = mybir.dt.uint32
U8 = mybir.dt.uint8
FP8X4 = mybir.dt.float8_e4m3fn_x4
ACT = mybir.ActivationFunctionType
ALU = mybir.AluOpType

P = 128
FEATURES = 512
OUTPUTS = 768
BASES = 2
PACK = 4
HALVES = 2
SPLINE_PASSES = 2
PASSES = 3
GROUP = 256
GROUPS = OUTPUTS // GROUP
ROWS = GROUP // P
WARM_UP = 8
CENTRES = (-1.0, 1.0)
HAT_SLOPE = 0.5

FLOPS = 2 * P * OUTPUTS * FEATURES * (1 + BASES)


def tile_generatorhead_pb_s_kernel(tc, h_norm, base_w2, spline_w2, out):
    nc = tc.nc
    x_dram = h_norm.flatten_outer_dims()
    out_dram = out.flatten_outer_dims()

    with ExitStack() as ctx:
        consts = ctx.enter_context(tc.tile_pool(name="consts", bufs=1))
        loaded = ctx.enter_context(tc.tile_pool(name="loaded", bufs=1))
        keep = ctx.enter_context(tc.tile_pool(name="keep", bufs=1))
        banks = ctx.enter_context(tc.psum_pool(name="banks", bufs=8))
        ctx.enter_context(tc.manual_schedule())

        x_rows = loaded.tile([P, FEATURES], BF16, name="x_rows")
        nc.sync.dma_start(out=x_rows[:], in_=x_dram)
        spline_rows = [loaded.tile([P, ROWS, FEATURES * BASES], BF16, name="spline_rows%d" % g) for g in range(GROUPS)]
        base_rows = [loaded.tile([P, ROWS, FEATURES], BF16, name="base_rows%d" % g) for g in range(GROUPS)]

        def load_spline(g, rows):
            source = spline_w2[g * GROUP : (g + 1) * GROUP, :, :].rearrange("(p r) i c -> p r (i c)", r=ROWS)
            nc.sync.dma_start(out=spline_rows[g][:, rows, :], in_=source[:, rows, :])

        def load_base(g):
            source = base_w2[g * GROUP : (g + 1) * GROUP, :].rearrange("(p r) i -> p r i", r=ROWS)
            nc.sync.dma_start(out=base_rows[g][:], in_=source)

        def load_last_base(r):
            first = (GROUPS - 1) * GROUP + r * P
            nc.sync.dma_start(out=base_rows[GROUPS - 1][:, r, :], in_=base_w2[first : first + P, :])

        load_base(0)
        load_spline(0, slice(0, ROWS))
        load_spline(1, slice(0, ROWS))
        load_base(1)
        for r in range(ROWS):
            load_spline(2, slice(r, r + 1))
        for r in range(ROWS):
            load_last_base(r)

        ident_f32 = consts.tile([P, P], F32, name="ident_f32")
        make_identity(nc, ident_f32[:])
        ident_bf16 = consts.tile([P, P], BF16, name="ident_bf16")
        make_identity(nc, ident_bf16[:])

        def quantise(grouped, name):
            n = grouped.shape[1] // PACK
            codes = keep.tile([P, n], U32, name="codes_" + name, align_bytes=64)
            scales = keep.tile([P, n], U8, name="scales_" + name, align_bytes=64)
            nc.vector.quantize_mx(out=codes[:].bitcast(FP8X4), scales=scales[:], in_=grouped)
            return codes, scales

        zeros = consts.tile([P, P * PACK], BF16, name="zeros", align_bytes=64)
        nc.vector.memset(zeros[:].bitcast(U32), 0)
        zero_codes, zero_scales = quantise(zeros[:], "zeros")
        minus_centre = consts.tile([P, BASES], F32, name="minus_centre")
        for c in range(BASES):
            nc.vector.memset(minus_centre[:, c : c + 1], -HAT_SLOPE * CENTRES[c])
        idle_bank = banks.tile([P, P], F32, tag="bank", name="idle_bank")
        for n in range(WARM_UP):
            nc.tensor.matmul_mx(
                out=idle_bank[:],
                lhsT=zero_codes[:].bitcast(FP8X4),
                lhsT_scale=zero_scales[:],
                rhs=zero_codes[:].bitcast(FP8X4),
                rhs_scale=zero_scales[:],
                start=True,
                stop=True,
            )

        x_words = banks.tile([P, HALVES * P], F32, tag="bank", name="x_words")
        for u in range(HALVES):
            nc.tensor.transpose(x_words[:, u * P : (u + 1) * P], x_rows[:].bitcast(F32)[:, u * P : (u + 1) * P], ident_f32[:])

        x_feats = banks.tile([P, SPLINE_PASSES * HALVES, P], BF16, tag="bank", name="x_feats")
        for f in range(SPLINE_PASSES * HALVES):
            nc.tensor.transpose(x_feats[:, f, :], x_rows[:, f * P : (f + 1) * P], ident_bf16[:])

        silu_grouped = keep.tile([P, P * PACK], BF16, name="silu_grouped", align_bytes=64)
        nc.scalar.activation(
            out=silu_grouped[:].rearrange("p (t u e) -> p t u e", u=HALVES, e=2),
            in_=x_words[:].bitcast(BF16).rearrange("p (u t e) -> p t u e", u=HALVES, e=2),
            func=ACT.Silu,
        )
        distance = keep.tile([P, BASES, FEATURES], F32, name="distance")
        for c in range(BASES):
            nc.scalar.activation(
                out=distance[:, c, :].rearrange("p (s t h) -> p s t h", s=SPLINE_PASSES, h=HALVES),
                in_=x_feats[:].rearrange("p (s h) t -> p s t h", h=HALVES),
                func=ACT.Abs,
                scale=HAT_SLOPE,
                bias=minus_centre[:, c : c + 1],
            )
        minus_silu = keep.tile([P, P * PACK], BF16, name="minus_silu", align_bytes=64)
        minus_hats = keep.tile([P, FEATURES * BASES], BF16, name="minus_hats", align_bytes=64)

        def negate_silu():
            nc.vector.tensor_scalar_mul(out=minus_silu[:], in0=silu_grouped[:], scalar1=-1.0)

        def finish_hats():
            nc.vector.tensor_scalar(
                out=minus_hats[:].rearrange("p (n c) -> p n c", c=BASES),
                in0=distance[:].rearrange("p c n -> p n c"),
                scalar1=1.0,
                scalar2=1.0,
                op0=ALU.min,
                op1=ALU.subtract,
            )

        x_codes = keep.tile([P, PASSES * P], U32, name="x_codes", align_bytes=64)
        x_scales = keep.tile([P, PASSES * P], U8, name="x_scales", align_bytes=64)

        def quantise_hats():
            cols = slice(0, SPLINE_PASSES * P)
            nc.vector.quantize_mx(out=x_codes[:, cols].bitcast(FP8X4), scales=x_scales[:, cols], in_=minus_hats[:])

        def quantise_silu():
            cols = slice(SPLINE_PASSES * P, PASSES * P)
            nc.vector.quantize_mx(out=x_codes[:, cols].bitcast(FP8X4), scales=x_scales[:, cols], in_=minus_silu[:])

        def spline_words(g, s):
            return spline_rows[g][:].rearrange("p r n -> p (r n)").bitcast(F32).rearrange("p (r s h k) -> p r s h k", r=ROWS, k=P, h=HALVES)[:, :, s, :, :]

        def base_words(g):
            return base_rows[g][:].rearrange("p r n -> p (r n)").bitcast(F32).rearrange("p (r h k) -> p r h k", r=ROWS, h=HALVES)

        def new_bank(rows):
            return banks.tile([P, rows * HALVES, P], F32, tag="bank", name="bank")

        def transpose_row(bank, b, words, r):
            for h in range(HALVES):
                nc.tensor.transpose(bank[:, b * HALVES + h, :], words[:, r, h, :], ident_f32[:])

        def transpose_rows(words):
            bank = new_bank(ROWS)
            for r in range(ROWS):
                transpose_row(bank, r, words, r)
            return bank

        def regroup(copy_out, bank, name):
            n = bank.shape[1]
            grouped = keep.tile([P, n * P * 2], BF16, name="grouped_" + name, align_bytes=64)
            copy_out(
                out=grouped[:].bitcast(F32).rearrange("k (p h) -> k p h", h=n),
                in_=bank[:].rearrange("k h p -> k p h"),
            )
            return grouped[:]

        def multiply(acc, c, operand, first=0):
            codes, scales = operand
            cols = slice(first, first + acc.shape[1])
            nc.tensor.matmul_mx(
                out=acc[:],
                lhsT=x_codes[:, c * P : (c + 1) * P].bitcast(FP8X4),
                lhsT_scale=x_scales[:, c * P : (c + 1) * P],
                rhs=codes[:, cols].bitcast(FP8X4),
                rhs_scale=scales[:, cols],
                start=(c == 0),
                stop=(c == PASSES - 1),
            )

        def multiply_group(operands):
            acc = banks.tile([P, GROUP], F32, tag="bank", name="acc")
            for c in range(PASSES):
                multiply(acc, c, operands[c])
            return acc

        def store(acc, g):
            result = keep.tile([P, GROUP], F32, name="result%d" % g)
            nc.scalar.activation(out=result[:], in_=acc[:], func=ACT.Copy, scale=-1.0)
            nc.sync.dma_start(out=out_dram[:, g * GROUP : (g + 1) * GROUP], in_=result[:])

        vec = nc.vector.tensor_copy
        sca = nc.scalar.copy
        negate_silu()
        g02 = regroup(vec, transpose_rows(base_words(0)), "02")
        quantise_silu()
        q02 = quantise(g02, "02")
        finish_hats()
        g00 = regroup(sca, transpose_rows(spline_words(0, 0)), "00")
        g01 = regroup(sca, transpose_rows(spline_words(0, 1)), "01")
        q00 = quantise(g00, "00")
        q01 = quantise(g01, "01")
        quantise_hats()
        g10 = regroup(sca, transpose_rows(spline_words(1, 0)), "10")
        g11 = regroup(vec, transpose_rows(spline_words(1, 1)), "11")
        g12 = regroup(sca, transpose_rows(base_words(1)), "12")
        q10 = quantise(g10, "10")
        q11 = quantise(g11, "11")
        q12 = quantise(g12, "12")
        spline_banks = [new_bank(ROWS) for c in range(SPLINE_PASSES)]
        for r in range(ROWS):
            for c in range(SPLINE_PASSES):
                transpose_row(spline_banks[c], r, spline_words(2, c), r)
        base_banks = [new_bank(1) for r in range(ROWS)]
        for r in range(ROWS):
            transpose_row(base_banks[r], 0, base_words(2), r)
        g20 = regroup(sca, spline_banks[0], "20")
        g21 = regroup(sca, spline_banks[1], "21")
        q20 = quantise(g20, "20")
        q21 = quantise(g21, "21")
        q22 = [quantise(regroup(sca, base_banks[r], "22_%d" % r), "22_%d" % r) for r in range(ROWS)]
        store(multiply_group((q00, q01, q02)), 0)
        store(multiply_group((q10, q11, q12)), 1)
        halves = [banks.tile([P, P], F32, tag="bank", name="half%d" % r) for r in range(ROWS)]
        for r in range(ROWS):
            multiply(halves[r], 0, q20, r * P)
            multiply(halves[r], 1, q21, r * P)
        for r in range(ROWS):
            multiply(halves[r], 2, q22[r])
        last = keep.tile([P, GROUP], F32, name="result_last")
        nc.scalar.activation(out=last[:, :P], in_=halves[0][:], func=ACT.Copy, scale=-1.0)
        nc.vector.tensor_scalar_mul(out=last[:, P:], in0=halves[1][:], scalar1=-1.0)
        nc.sync.dma_start(out=out_dram[:, 2 * GROUP :], in_=last[:])
